import numpy as np
import ml_dtypes


def mxq(x, axis, fmt="e4m3"):
    dtype, down = {"e4m3": (ml_dtypes.float8_e4m3fn, 7), "e5m2": (ml_dtypes.float8_e5m2, 14)}[fmt]
    v = np.moveaxis(np.asarray(x, np.float32).astype(ml_dtypes.bfloat16).astype(np.float64), axis, -1)
    blocks = v.reshape(v.shape[:-1] + (-1, 32))
    amax = np.abs(blocks).max(-1, keepdims=True)
    byte = np.maximum(np.where(amax > 0, np.frexp(amax)[1] - 1 + 127, 0) - down, 1)
    scale = np.exp2(byte - 127.0)
    codes = (blocks / scale).astype(np.float32).astype(dtype).astype(np.float64)
    return np.moveaxis((codes * scale).reshape(v.shape), -1, axis)


WIDE = False


def mx_kscale(k):
    if not WIDE:
        return np.ones(k)
    levels = np.array([10, -10, 5, -5, 0])
    a = np.random.permutation(np.resize(levels, k // 512 * 4)).reshape(k // 512, 4)
    idx = np.arange(k)
    return np.exp2(a[idx // 512, idx % 128 // 32])


BF16 = ml_dtypes.bfloat16


def bf(x):
    return np.asarray(x, np.float32).astype(BF16)


def f64(x):
    return np.asarray(x).astype(np.float64)


E2M1 = np.array([0.0, 0.5, 1.0, 1.5, 2.0, 3.0, 4.0, 6.0, -0.0, -0.5, -1.0, -1.5, -2.0, -3.0, -4.0, -6.0])


def pack_weight(w, fmt):
    k, n = w.shape
    w = f64(bf(w)).reshape(k // 32, 32, n)
    amax = np.abs(w).max(1)
    if fmt == "e4m3":
        byte = np.frexp(amax)[1] - 1 + 127 - 7
    else:
        mant, ex = np.frexp(amax / 6.0)
        byte = np.where(mant > 0.5, ex, ex - 1) + 127
    byte = np.clip(np.where(amax > 0, byte, 1), 1, 254)
    scaled = (w * np.exp2(127.0 - byte)[:, None, :]).reshape(k, n).astype(np.float32)
    by_word = np.ascontiguousarray(scaled.reshape(k // 512, 128, 4, n).transpose(0, 1, 3, 2))
    if fmt == "e4m3":
        words = by_word.astype(ml_dtypes.float8_e4m3fn).view(np.uint8)
    else:
        c = by_word.astype(ml_dtypes.float4_e2m1fn).view(np.uint8) & 0xF
        words = c[..., 0::2] | (c[..., 1::2] << 4)
    return np.ascontiguousarray(words), np.ascontiguousarray(byte.astype(np.uint8).reshape(k // 512, 16, n))


def unpack_weight(words, scales, fmt):
    g, p, n, _ = words.shape
    if fmt == "e4m3":
        vals = np.ascontiguousarray(words).view(ml_dtypes.float8_e4m3fn).astype(np.float64)
    else:
        nib = np.empty((g, p, n, 4), np.uint8)
        nib[..., 0::2] = words & 0xF
        nib[..., 1::2] = words >> 4
        vals = E2M1[nib]
    vals = vals * np.repeat(np.exp2(scales.astype(np.float64) - 127.0), 8, axis=1)[..., None]
    return vals.transpose(0, 1, 3, 2).reshape(g * 512, n)


B, S, HIDDEN, NUM_HEADS, HEAD_DIM = 1, 128, 16384, 16, 32
F = NUM_HEADS * HEAD_DIM
FMT = "e4m3"


def _split_heads(x):
    b, s, _ = x.shape
    return x.reshape(b, s, NUM_HEADS, HEAD_DIM).transpose(0, 2, 1, 3)


def setup_inputs():
    s = mx_kscale(HIDDEN)
    scale = 1.0 / np.sqrt(HIDDEN)
    hidden_states = bf(np.random.standard_normal((B, S, HIDDEN)) * s)
    Wq_words, Wq_scales = pack_weight(np.random.standard_normal((HIDDEN, F)) * scale / s[:, None], FMT)
    bq = bf(np.random.standard_normal(F) * 0.5)
    Wk_words, Wk_scales = pack_weight(np.random.standard_normal((HIDDEN, F)) * scale / s[:, None], FMT)
    bk = bf(np.random.standard_normal(F) * 0.5)
    Wv_words, Wv_scales = pack_weight(np.random.standard_normal((HIDDEN, F)) * scale / s[:, None], FMT)
    bv = bf(np.random.standard_normal(F) * 0.5)
    return {
        "hidden_states": hidden_states,
        "Wq_words": Wq_words,
        "Wq_scales": Wq_scales,
        "bq": bq,
        "Wk_words": Wk_words,
        "Wk_scales": Wk_scales,
        "bk": bk,
        "Wv_words": Wv_words,
        "Wv_scales": Wv_scales,
        "bv": bv,
    }


def reference(hidden_states, Wq_words, Wq_scales, bq, Wk_words, Wk_scales, bk, Wv_words, Wv_scales, bv):
    Wqkv = np.concatenate([
        unpack_weight(Wq_words, Wq_scales, FMT),
        unpack_weight(Wk_words, Wk_scales, FMT),
        unpack_weight(Wv_words, Wv_scales, FMT),
    ], axis=1)
    bqkv = np.concatenate([f64(bq), f64(bk), f64(bv)], axis=0)
    qkv = (mxq(f64(hidden_states), 2, "e4m3") @ Wqkv) + bqkv
    q, k, v = np.split(qkv, 3, axis=-1)
    return (_split_heads(q), _split_heads(k), _split_heads(v))

@@ -1,0 +1,170 @@
+from contextlib import ExitStack
+
+import concourse.mybir as mybir
+from concourse.masks import make_identity
+
+BF16 = mybir.dt.bfloat16
+F32 = mybir.dt.float32
+I32 = mybir.dt.int32
+U32 = mybir.dt.uint32
+U8 = mybir.dt.uint8
+FP8X4 = mybir.dt.float8_e4m3fn_x4
+
+P = 128
+HIDDEN = 16384
+FEATURES = 512
+HEADS = 16
+HEAD_DIM = 32
+PACK = 4
+BLOCK = 32
+POSITIONS = 16
+QUARTERS = 4
+PASSES = 8
+QUARTER_K = HIDDEN // QUARTERS
+WORDS_PER_PASS = POSITIONS * BLOCK // 2
+PASSES_PER_BANK = 2
+WEIGHT_SLOTS = 32
+
+FLOPS = 2 * P * HIDDEN * 3 * FEATURES
+
+
+def tile_attention_before_k_kernel(
+    tc,
+    hidden_states,
+    Wq_words,
+    Wq_scales,
+    bq,
+    Wk_words,
+    Wk_scales,
+    bk,
+    Wv_words,
+    Wv_scales,
+    bv,
+    out_0,
+    out_1,
+    out_2,
+):
+    nc = tc.nc
+    x = hidden_states.rearrange("b s k -> (b s) k")
+    biases = [bq, bk, bv]
+    outs = [o.rearrange("b h s d -> s (b h) d") for o in (out_0, out_1, out_2)]
+    word_rows = [
+        w.rearrange("g p n t -> (g p) (n t)").rearrange(
+            "(j pos c i) b -> j c pos i b", j=QUARTERS, pos=POSITIONS, c=PASSES
+        )
+        for w in (Wq_words, Wk_words, Wv_words)
+    ]
+    scale_runs = [
+        s.rearrange("g q n -> (g q n)").rearrange(
+            "(j quad r b) -> quad j r b", j=QUARTERS, quad=4, r=4
+        )
+        for s in (Wq_scales, Wk_scales, Wv_scales)
+    ]
+
+    with ExitStack() as ctx:
+        ctx.enter_context(tc.manual_schedule())
+        keep = ctx.enter_context(tc.tile_pool(name="keep", bufs=1))
+        x_pool = ctx.enter_context(tc.tile_pool(name="x_pool", bufs=QUARTERS))
+        grouped_pool = ctx.enter_context(tc.tile_pool(name="grouped_pool", bufs=2))
+        weight_pool = ctx.enter_context(tc.tile_pool(name="weight_pool", bufs=WEIGHT_SLOTS))
+        transposed_pool = ctx.enter_context(tc.psum_pool(name="transposed_pool", bufs=4))
+        sum_pool = ctx.enter_context(tc.psum_pool(name="sum_pool", bufs=1))
+
+        x_raw = []
+        for j in range(QUARTERS):
+            raw = x_pool.tile([P, QUARTER_K], BF16, name="x_raw")
+            nc.sync.dma_start(out=raw[:], in_=x[:, j * QUARTER_K : (j + 1) * QUARTER_K])
+            x_raw.append(raw)
+
+        bias_rows = keep.tile([P, 3 * FEATURES], BF16)
+        nc.vector.memset(bias_rows[:], 0.0)
+        ones = keep.tile([P, P], BF16)
+        nc.vector.memset(ones[:], 1.0)
+        identity = keep.tile([P, P], F32)
+        make_identity(nc, identity[:])
+        for w in range(3):
+            nc.scalar.dma_start(
+                out=bias_rows[0:1, w * FEATURES : (w + 1) * FEATURES],
+                in_=biases[w].rearrange("(o n) -> o n", o=1),
+            )
+        bias_all = keep.tile([P, 3, FEATURES], F32)
+        for w in range(3):
+            bias_sum = sum_pool.tile([P, FEATURES], F32, name="bias_sum", tag="bank%d" % w)
+            nc.tensor.matmul(
+                out=bias_sum[:],
+                lhsT=ones[:],
+                rhs=bias_rows[:, w * FEATURES : (w + 1) * FEATURES],
+                start=True,
+                stop=True,
+            )
+            nc.scalar.copy(out=bias_all[:, w, :], in_=bias_sum[:])
+
+        w_scales = []
+        for w in range(3):
+            planes = keep.tile([P, PASSES * FEATURES], U8, name="w_scales%d" % w, align_bytes=64)
+            nc.vector.memset(planes[:].bitcast(I32), 0)
+            w_scales.append(planes)
+        for w in range(3):
+            for quad in range(4):
+                nc.sync.dma_start(
+                    out=w_scales[w][32 * quad : 32 * quad + 16, :].bitcast(I32),
+                    in_=scale_runs[w][quad].bitcast(I32),
+                )
+
+        x_sorted = []
+        for j in range(QUARTERS):
+            by_pass = x_pool.tile([P, QUARTER_K], BF16, name="x_sorted")
+            nc.vector.tensor_copy(
+                out=by_pass[:].rearrange("m (c pos e) -> m c pos e", c=PASSES, pos=POSITIONS),
+                in_=x_raw[j][:].rearrange("m (pos c e) -> m c pos e", pos=POSITIONS, c=PASSES),
+            )
+            x_sorted.append(by_pass)
+
+        x_codes = keep.tile([P, QUARTERS * PASSES, P], U32, align_bytes=64)
+        x_scales = keep.tile([P, QUARTERS * PASSES, P], U8, align_bytes=64)
+        for j in range(QUARTERS):
+            words = x_sorted[j][:].bitcast(F32)
+            grouped = grouped_pool.tile([P, PASSES, P, PACK], BF16, align_bytes=64)
+            for first in range(0, PASSES, PASSES_PER_BANK):
+                transposed = transposed_pool.tile([P, PASSES_PER_BANK, 2, P], F32)
+                for c in range(first, first + PASSES_PER_BANK):
+                    for half in range(2):
+                        nc.tensor.transpose(
+                            out=transposed[:, c - first, half, :],
+                            in_=words[:, c * WORDS_PER_PASS + half : (c + 1) * WORDS_PER_PASS : 2],
+                            identity=identity[:],
+                        )
+                nc.scalar.copy(
+                    out=grouped[:, first : first + PASSES_PER_BANK, :, :].bitcast(F32),
+                    in_=transposed[:].rearrange("p c half m -> p c m half"),
+                )
+            nc.vector.quantize_mx(
+                out=x_codes[:, j * PASSES : (j + 1) * PASSES, :]
+                .rearrange("p c m -> p (c m)")
+                .bitcast(FP8X4),
+                scales=x_scales[:, j * PASSES : (j + 1) * PASSES, :].rearrange("p c m -> p (c m)"),
+                in_=grouped[:].rearrange("p c m t -> p (c m t)"),
+            )
+
+        for w in range(3):
+            total = sum_pool.tile([P, FEATURES], F32, name="total", tag="bank%d" % w)
+            for j in range(QUARTERS):
+                for c in range(PASSES):
+                    w_codes = weight_pool.tile([P, FEATURES], U32, align_bytes=64)
+                    nc.sync.dma_start(out=w_codes[:].bitcast(I32), in_=word_rows[w][j, c].bitcast(I32))
+                    nc.tensor.matmul_mx(
+                        out=total[:],
+                        lhsT=x_codes[:, j * PASSES + c, :].bitcast(FP8X4),
+                        lhsT_scale=x_scales[:, j * PASSES + c, :],
+                        rhs=w_codes[:].bitcast(FP8X4),
+                        rhs_scale=w_scales[w][4 * j : P, c * FEATURES : (c + 1) * FEATURES],
+                        start=(j == 0 and c == 0),
+                        stop=(j == QUARTERS - 1 and c == PASSES - 1),
+                    )
+            result = keep.tile([P, FEATURES], F32, name="result%d" % w)
+            nc.vector.tensor_tensor(
+                out=result[:], in0=total[:], in1=bias_all[:, w, :], op=mybir.AluOpType.add
+            )
+            nc.scalar.dma_start(
+                out=outs[w], in_=result[:].rearrange("s (h d) -> s h d", h=HEADS)
+            )

@@ -14,16 +14,17 @@ P = 128
 HIDDEN = 16384
 FEATURES = 512
 HEADS = 16
-HEAD_DIM = 32
 PACK = 4
-BLOCK = 32
-POSITIONS = 16
-QUARTERS = 4
-PASSES = 8
-QUARTER_K = HIDDEN // QUARTERS
-WORDS_PER_PASS = POSITIONS * BLOCK // 2
-PASSES_PER_BANK = 2
-WEIGHT_SLOTS = 32
+GROUP_K = P * PACK
+GROUPS = HIDDEN // GROUP_K
+X_PIECES = 4
+X_GROUPS = GROUPS // X_PIECES
+GROUP_WORDS = GROUP_K // 2
+GROUPS_PER_BANK = 2
+LOAD_GROUPS = 4
+WEIGHT_SLOTS = 10
+PLANES = 4
+PLANE_GROUPS = GROUPS // PLANES
 
 FLOPS = 2 * P * HIDDEN * 3 * FEATURES
 
@@ -47,33 +48,25 @@ def tile_attention_before_k_kernel(
     nc = tc.nc
     x = hidden_states.rearrange("b s k -> (b s) k")
     biases = [bq, bk, bv]
+    scale_bytes = [Wq_scales, Wk_scales, Wv_scales]
     outs = [o.rearrange("b h s d -> s (b h) d") for o in (out_0, out_1, out_2)]
-    word_rows = [
-        w.rearrange("g p n t -> (g p) (n t)").rearrange(
-            "(j pos c i) b -> j c pos i b", j=QUARTERS, pos=POSITIONS, c=PASSES
-        )
-        for w in (Wq_words, Wk_words, Wv_words)
-    ]
-    scale_runs = [
-        s.rearrange("g q n -> (g q n)").rearrange(
-            "(j quad r b) -> quad j r b", j=QUARTERS, quad=4, r=4
-        )
-        for s in (Wq_scales, Wk_scales, Wv_scales)
-    ]
+    word_rows = [w.rearrange("g p n t -> p g (n t)") for w in (Wq_words, Wk_words, Wv_words)]
 
     with ExitStack() as ctx:
         ctx.enter_context(tc.manual_schedule())
         keep = ctx.enter_context(tc.tile_pool(name="keep", bufs=1))
-        x_pool = ctx.enter_context(tc.tile_pool(name="x_pool", bufs=QUARTERS))
+        x_pool = ctx.enter_context(tc.tile_pool(name="x_pool", bufs=X_PIECES))
         grouped_pool = ctx.enter_context(tc.tile_pool(name="grouped_pool", bufs=2))
         weight_pool = ctx.enter_context(tc.tile_pool(name="weight_pool", bufs=WEIGHT_SLOTS))
         transposed_pool = ctx.enter_context(tc.psum_pool(name="transposed_pool", bufs=4))
         sum_pool = ctx.enter_context(tc.psum_pool(name="sum_pool", bufs=1))
 
         x_raw = []
-        for j in range(QUARTERS):
-            raw = x_pool.tile([P, QUARTER_K], BF16, name="x_raw")
-            nc.sync.dma_start(out=raw[:], in_=x[:, j * QUARTER_K : (j + 1) * QUARTER_K])
+        for piece in range(X_PIECES):
+            raw = x_pool.tile([P, X_GROUPS * GROUP_K], BF16, name="x_raw")
+            nc.sync.dma_start(
+                out=raw[:], in_=x[:, piece * X_GROUPS * GROUP_K : (piece + 1) * X_GROUPS * GROUP_K]
+            )
             x_raw.append(raw)
 
         bias_rows = keep.tile([P, 3 * FEATURES], BF16)
@@ -87,6 +80,49 @@ def tile_attention_before_k_kernel(
                 out=bias_rows[0:1, w * FEATURES : (w + 1) * FEATURES],
                 in_=biases[w].rearrange("(o n) -> o n", o=1),
             )
+
+        w_scales = []
+        for w in range(3):
+            planes = keep.tile([P, PLANE_GROUPS * FEATURES], U8, name="w_scales%d" % w, align_bytes=64)
+            nc.vector.memset(planes[:].bitcast(I32), 0)
+            w_scales.append(planes)
+        for w in range(3):
+            for quad in range(4):
+                for r in range(4):
+                    nc.gpsimd.dma_start(
+                        out=w_scales[w][32 * quad + r : 32 * quad + 4 * PLANES : 4, :]
+                        .bitcast(F32)
+                        .rearrange("plane (g n) -> plane g n", g=PLANE_GROUPS),
+                        in_=scale_bytes[w][:, 4 * quad + r, :]
+                        .rearrange("(plane g) n -> plane g n", plane=PLANES)
+                        .bitcast(F32),
+                    )
+
+        x_codes = keep.tile([P, GROUPS, P], U32, align_bytes=64)
+        x_scales = keep.tile([P, GROUPS, P], U8, align_bytes=64)
+        for piece in range(X_PIECES):
+            words = x_raw[piece][:].bitcast(F32)
+            grouped = grouped_pool.tile([P, X_GROUPS, P, PACK], BF16, align_bytes=64)
+            for first in range(0, X_GROUPS, GROUPS_PER_BANK):
+                transposed = transposed_pool.tile([P, GROUPS_PER_BANK, 2, P], F32)
+                for g in range(first, first + GROUPS_PER_BANK):
+                    for half in range(2):
+                        nc.tensor.transpose(
+                            out=transposed[:, g - first, half, :],
+                            in_=words[:, g * GROUP_WORDS + half : (g + 1) * GROUP_WORDS : 2],
+                            identity=identity[:],
+                        )
+                nc.scalar.copy(
+                    out=grouped[:, first : first + GROUPS_PER_BANK, :, :].bitcast(F32),
+                    in_=transposed[:].rearrange("p g half m -> p g m half"),
+                )
+            piece_groups = slice(piece * X_GROUPS, (piece + 1) * X_GROUPS)
+            nc.vector.quantize_mx(
+                out=x_codes[:, piece_groups, :].rearrange("p g m -> p (g m)").bitcast(FP8X4),
+                scales=x_scales[:, piece_groups, :].rearrange("p g m -> p (g m)"),
+                in_=grouped[:].rearrange("p g m t -> p (g m t)"),
+            )
+
         bias_all = keep.tile([P, 3, FEATURES], F32)
         for w in range(3):
             bias_sum = sum_pool.tile([P, FEATURES], F32, name="bias_sum", tag="bank%d" % w)
@@ -99,72 +135,28 @@ def tile_attention_before_k_kernel(
             )
             nc.scalar.copy(out=bias_all[:, w, :], in_=bias_sum[:])
 
-        w_scales = []
-        for w in range(3):
-            planes = keep.tile([P, PASSES * FEATURES], U8, name="w_scales%d" % w, align_bytes=64)
-            nc.vector.memset(planes[:].bitcast(I32), 0)
-            w_scales.append(planes)
-        for w in range(3):
-            for quad in range(4):
-                nc.sync.dma_start(
-                    out=w_scales[w][32 * quad : 32 * quad + 16, :].bitcast(I32),
-                    in_=scale_runs[w][quad].bitcast(I32),
-                )
-
-        x_sorted = []
-        for j in range(QUARTERS):
-            by_pass = x_pool.tile([P, QUARTER_K], BF16, name="x_sorted")
-            nc.vector.tensor_copy(
-                out=by_pass[:].rearrange("m (c pos e) -> m c pos e", c=PASSES, pos=POSITIONS),
-                in_=x_raw[j][:].rearrange("m (pos c e) -> m c pos e", pos=POSITIONS, c=PASSES),
-            )
-            x_sorted.append(by_pass)
-
-        x_codes = keep.tile([P, QUARTERS * PASSES, P], U32, align_bytes=64)
-        x_scales = keep.tile([P, QUARTERS * PASSES, P], U8, align_bytes=64)
-        for j in range(QUARTERS):
-            words = x_sorted[j][:].bitcast(F32)
-            grouped = grouped_pool.tile([P, PASSES, P, PACK], BF16, align_bytes=64)
-            for first in range(0, PASSES, PASSES_PER_BANK):
-                transposed = transposed_pool.tile([P, PASSES_PER_BANK, 2, P], F32)
-                for c in range(first, first + PASSES_PER_BANK):
-                    for half in range(2):
-                        nc.tensor.transpose(
-                            out=transposed[:, c - first, half, :],
-                            in_=words[:, c * WORDS_PER_PASS + half : (c + 1) * WORDS_PER_PASS : 2],
-                            identity=identity[:],
-                        )
-                nc.scalar.copy(
-                    out=grouped[:, first : first + PASSES_PER_BANK, :, :].bitcast(F32),
-                    in_=transposed[:].rearrange("p c half m -> p c m half"),
-                )
-            nc.vector.quantize_mx(
-                out=x_codes[:, j * PASSES : (j + 1) * PASSES, :]
-                .rearrange("p c m -> p (c m)")
-                .bitcast(FP8X4),
-                scales=x_scales[:, j * PASSES : (j + 1) * PASSES, :].rearrange("p c m -> p (c m)"),
-                in_=grouped[:].rearrange("p c m t -> p (c m t)"),
-            )
-
         for w in range(3):
             total = sum_pool.tile([P, FEATURES], F32, name="total", tag="bank%d" % w)
-            for j in range(QUARTERS):
-                for c in range(PASSES):
-                    w_codes = weight_pool.tile([P, FEATURES], U32, align_bytes=64)
-                    nc.sync.dma_start(out=w_codes[:].bitcast(I32), in_=word_rows[w][j, c].bitcast(I32))
+            for first in range(0, GROUPS, LOAD_GROUPS):
+                w_codes = weight_pool.tile([P, LOAD_GROUPS, FEATURES], U32, align_bytes=64)
+                nc.sync.dma_start(
+                    out=w_codes[:].bitcast(I32),
+                    in_=word_rows[w][:, first : first + LOAD_GROUPS, :].bitcast(I32),
+                )
+                for g in range(first, first + LOAD_GROUPS):
+                    plane = g // PLANE_GROUPS
+                    column = (g % PLANE_GROUPS) * FEATURES
                     nc.tensor.matmul_mx(
                         out=total[:],
-                        lhsT=x_codes[:, j * PASSES + c, :].bitcast(FP8X4),
-                        lhsT_scale=x_scales[:, j * PASSES + c, :],
-                        rhs=w_codes[:].bitcast(FP8X4),
-                        rhs_scale=w_scales[w][4 * j : P, c * FEATURES : (c + 1) * FEATURES],
-                        start=(j == 0 and c == 0),
-                        stop=(j == QUARTERS - 1 and c == PASSES - 1),
+                        lhsT=x_codes[:, g, :].bitcast(FP8X4),
+                        lhsT_scale=x_scales[:, g, :],
+                        rhs=w_codes[:, g - first, :].bitcast(FP8X4),
+                        rhs_scale=w_scales[w][4 * plane : P, column : column + FEATURES],
+                        start=(g == 0),
+                        stop=(g == GROUPS - 1),
                     )
             result = keep.tile([P, FEATURES], F32, name="result%d" % w)
             nc.vector.tensor_tensor(
                 out=result[:], in0=total[:], in1=bias_all[:, w, :], op=mybir.AluOpType.add
             )
-            nc.scalar.dma_start(
-                out=outs[w], in_=result[:].rearrange("s (h d) -> s h d", h=HEADS)
-            )
+            nc.scalar.dma_start(out=outs[w], in_=result[:].rearrange("s (h d) -> s h d", h=HEADS))

@@ -25,6 +25,9 @@ LOAD_GROUPS = 4
 WEIGHT_SLOTS = 10
 PLANES = 4
 PLANE_GROUPS = GROUPS // PLANES
+RESULT_PIECES = 2
+PIECE_HEADS = HEADS // RESULT_PIECES
+PIECE_COLUMNS = FEATURES // RESULT_PIECES
 
 FLOPS = 2 * P * HIDDEN * 3 * FEATURES
 
@@ -139,10 +142,13 @@ def tile_attention_before_k_kernel(
             total = sum_pool.tile([P, FEATURES], F32, name="total", tag="bank%d" % w)
             for first in range(0, GROUPS, LOAD_GROUPS):
                 w_codes = weight_pool.tile([P, LOAD_GROUPS, FEATURES], U32, align_bytes=64)
-                nc.sync.dma_start(
-                    out=w_codes[:].bitcast(I32),
-                    in_=word_rows[w][:, first : first + LOAD_GROUPS, :].bitcast(I32),
-                )
+                last_load = w == 2 and first == GROUPS - LOAD_GROUPS
+                cut = 1 if last_load else LOAD_GROUPS
+                for part in range(0, LOAD_GROUPS, cut):
+                    nc.sync.dma_start(
+                        out=w_codes[:, part : part + cut, :].bitcast(I32),
+                        in_=word_rows[w][:, first + part : first + part + cut, :].bitcast(I32),
+                    )
                 for g in range(first, first + LOAD_GROUPS):
                     plane = g // PLANE_GROUPS
                     column = (g % PLANE_GROUPS) * FEATURES
@@ -155,8 +161,17 @@ def tile_attention_before_k_kernel(
                         start=(g == 0),
                         stop=(g == GROUPS - 1),
                     )
+            store_queue = nc.sync if w == 2 else nc.scalar
             result = keep.tile([P, FEATURES], F32, name="result%d" % w)
-            nc.vector.tensor_tensor(
-                out=result[:], in0=total[:], in1=bias_all[:, w, :], op=mybir.AluOpType.add
-            )
-            nc.scalar.dma_start(out=outs[w], in_=result[:].rearrange("s (h d) -> s h d", h=HEADS))
+            for piece in range(RESULT_PIECES):
+                columns = slice(piece * PIECE_COLUMNS, (piece + 1) * PIECE_COLUMNS)
+                nc.vector.tensor_tensor(
+                    out=result[:, columns],
+                    in0=total[:, columns],
+                    in1=bias_all[:, w, columns],
+                    op=mybir.AluOpType.add,
+                )
+                store_queue.dma_start(
+                    out=outs[w][:, piece * PIECE_HEADS : (piece + 1) * PIECE_HEADS, :],
+                    in_=result[:, columns].rearrange("s (h d) -> s h d", h=PIECE_HEADS),
+                )

@@ -138,6 +138,7 @@ def tile_attention_before_k_kernel(
             )
             nc.scalar.copy(out=bias_all[:, w, :], in_=bias_sum[:])
 
+        results = []
         for w in range(3):
             total = sum_pool.tile([P, FEATURES], F32, name="total", tag="bank%d" % w)
             for first in range(0, GROUPS, LOAD_GROUPS):
@@ -161,8 +162,8 @@ def tile_attention_before_k_kernel(
                         start=(g == 0),
                         stop=(g == GROUPS - 1),
                     )
-            store_queue = nc.sync if w == 2 else nc.scalar
             result = keep.tile([P, FEATURES], F32, name="result%d" % w)
+            results.append(result)
             for piece in range(RESULT_PIECES):
                 columns = slice(piece * PIECE_COLUMNS, (piece + 1) * PIECE_COLUMNS)
                 nc.vector.tensor_tensor(
@@ -171,7 +172,11 @@ def tile_attention_before_k_kernel(
                     in1=bias_all[:, w, columns],
                     op=mybir.AluOpType.add,
                 )
-                store_queue.dma_start(
+
+        for w in range(3):
+            for piece in range(RESULT_PIECES):
+                columns = slice(piece * PIECE_COLUMNS, (piece + 1) * PIECE_COLUMNS)
+                nc.sync.dma_start(
                     out=outs[w][:, piece * PIECE_HEADS : (piece + 1) * PIECE_HEADS, :],
-                    in_=result[:, columns].rearrange("s (h d) -> s h d", h=PIECE_HEADS),
+                    in_=results[w][:, columns].rearrange("s (h d) -> s h d", h=PIECE_HEADS),
                 )

@@ -13,7 +13,6 @@ FP8X4 = mybir.dt.float8_e4m3fn_x4
 P = 128
 HIDDEN = 16384
 FEATURES = 512
-HEADS = 16
 PACK = 4
 GROUP_K = P * PACK
 GROUPS = HIDDEN // GROUP_K
@@ -25,9 +24,9 @@ LOAD_GROUPS = 4
 WEIGHT_SLOTS = 10
 PLANES = 4
 PLANE_GROUPS = GROUPS // PLANES
-RESULT_PIECES = 2
-PIECE_HEADS = HEADS // RESULT_PIECES
-PIECE_COLUMNS = FEATURES // RESULT_PIECES
+BLOCKS = FEATURES // P
+SQUARE = 32
+RUN = P // SQUARE
 
 FLOPS = 2 * P * HIDDEN * 3 * FEATURES
 
@@ -52,7 +51,10 @@ def tile_attention_before_k_kernel(
     x = hidden_states.rearrange("b s k -> (b s) k")
     biases = [bq, bk, bv]
     scale_bytes = [Wq_scales, Wk_scales, Wv_scales]
-    outs = [o.rearrange("b h s d -> s (b h) d") for o in (out_0, out_1, out_2)]
+    outs = [
+        o.rearrange("b h (a r) d -> (b h a) (r d)", r=RUN).rearrange("(c p) e -> p c e", p=P)
+        for o in (out_0, out_1, out_2)
+    ]
     word_rows = [w.rearrange("g p n t -> p g (n t)") for w in (Wq_words, Wk_words, Wv_words)]
 
     with ExitStack() as ctx:
@@ -72,16 +74,19 @@ def tile_attention_before_k_kernel(
             )
             x_raw.append(raw)
 
-        bias_rows = keep.tile([P, 3 * FEATURES], BF16)
+        bias_rows = keep.tile([P, P], BF16)
         nc.vector.memset(bias_rows[:], 0.0)
-        ones = keep.tile([P, P], BF16)
-        nc.vector.memset(ones[:], 1.0)
         identity = keep.tile([P, P], F32)
         make_identity(nc, identity[:])
+        reorder = keep.tile([P, P], F32)
+        nc.vector.tensor_copy(
+            out=reorder[:].rearrange("p (r a) -> p r a", r=RUN),
+            in_=identity[:].rearrange("p (a r) -> p r a", r=RUN),
+        )
         for w in range(3):
             nc.scalar.dma_start(
-                out=bias_rows[0:1, w * FEATURES : (w + 1) * FEATURES],
-                in_=biases[w].rearrange("(o n) -> o n", o=1),
+                out=bias_rows[w * BLOCKS : (w + 1) * BLOCKS, :],
+                in_=biases[w].rearrange("(c n) -> c n", c=BLOCKS),
             )
 
         w_scales = []
@@ -107,13 +112,13 @@ def tile_attention_before_k_kernel(
             words = x_raw[piece][:].bitcast(F32)
             grouped = grouped_pool.tile([P, X_GROUPS, P, PACK], BF16, align_bytes=64)
             for first in range(0, X_GROUPS, GROUPS_PER_BANK):
-                transposed = transposed_pool.tile([P, GROUPS_PER_BANK, 2, P], F32)
+                transposed = transposed_pool.tile([P, GROUPS_PER_BANK, 2, P], F32, name="transposed", tag="turned")
                 for g in range(first, first + GROUPS_PER_BANK):
                     for half in range(2):
                         nc.tensor.transpose(
                             out=transposed[:, g - first, half, :],
                             in_=words[:, g * GROUP_WORDS + half : (g + 1) * GROUP_WORDS : 2],
-                            identity=identity[:],
+                            identity=reorder[:],
                         )
                 nc.scalar.copy(
                     out=grouped[:, first : first + GROUPS_PER_BANK, :, :].bitcast(F32),
@@ -126,21 +131,19 @@ def tile_attention_before_k_kernel(
                 in_=grouped[:].rearrange("p g m t -> p (g m t)"),
             )
 
-        bias_all = keep.tile([P, 3, FEATURES], F32)
-        for w in range(3):
-            bias_sum = sum_pool.tile([P, FEATURES], F32, name="bias_sum", tag="bank%d" % w)
-            nc.tensor.matmul(
-                out=bias_sum[:],
-                lhsT=ones[:],
-                rhs=bias_rows[:, w * FEATURES : (w + 1) * FEATURES],
-                start=True,
-                stop=True,
-            )
-            nc.scalar.copy(out=bias_all[:, w, :], in_=bias_sum[:])
+        bias_words = keep.tile([P, P], F32)
+        nc.vector.tensor_copy(out=bias_words[:], in_=bias_rows[:])
+        bias_turned = transposed_pool.tile([P, P], F32, name="bias_turned", tag="turned")
+        nc.tensor.transpose(out=bias_turned[:], in_=bias_words[:], identity=identity[:])
+        bias_columns = keep.tile([P, 3 * BLOCKS], F32)
+        nc.vector.tensor_copy(out=bias_columns[:], in_=bias_turned[:, 0 : 3 * BLOCKS])
 
         results = []
         for w in range(3):
-            total = sum_pool.tile([P, FEATURES], F32, name="total", tag="bank%d" % w)
+            totals = []
+            for c in range(BLOCKS):
+                bank = sum_pool.tile([P, FEATURES], F32, name="bank", tag="bank%d" % c)
+                totals.append(bank[:, 0:P])
             for first in range(0, GROUPS, LOAD_GROUPS):
                 w_codes = weight_pool.tile([P, LOAD_GROUPS, FEATURES], U32, align_bytes=64)
                 last_load = w == 2 and first == GROUPS - LOAD_GROUPS
@@ -153,30 +156,29 @@ def tile_attention_before_k_kernel(
                 for g in range(first, first + LOAD_GROUPS):
                     plane = g // PLANE_GROUPS
                     column = (g % PLANE_GROUPS) * FEATURES
-                    nc.tensor.matmul_mx(
-                        out=total[:],
-                        lhsT=x_codes[:, g, :].bitcast(FP8X4),
-                        lhsT_scale=x_scales[:, g, :],
-                        rhs=w_codes[:, g - first, :].bitcast(FP8X4),
-                        rhs_scale=w_scales[w][4 * plane : P, column : column + FEATURES],
-                        start=(g == 0),
-                        stop=(g == GROUPS - 1),
-                    )
-            result = keep.tile([P, FEATURES], F32, name="result%d" % w)
+                    for c in range(BLOCKS):
+                        nc.tensor.matmul_mx(
+                            out=totals[c],
+                            lhsT=w_codes[:, g - first, c * P : (c + 1) * P].bitcast(FP8X4),
+                            lhsT_scale=w_scales[w][4 * plane : P, column + c * P : column + (c + 1) * P],
+                            rhs=x_codes[:, g, :].bitcast(FP8X4),
+                            rhs_scale=x_scales[:, g, :],
+                            start=(g == 0),
+                            stop=(g == GROUPS - 1),
+                        )
+            biased = keep.tile([P, BLOCKS, P], F32, name="biased%d" % w, align_bytes=64)
+            result = keep.tile([P, BLOCKS, P], F32, name="result%d" % w, align_bytes=64)
             results.append(result)
-            for piece in range(RESULT_PIECES):
-                columns = slice(piece * PIECE_COLUMNS, (piece + 1) * PIECE_COLUMNS)
-                nc.vector.tensor_tensor(
-                    out=result[:, columns],
-                    in0=total[:, columns],
-                    in1=bias_all[:, w, columns],
-                    op=mybir.AluOpType.add,
+            for c in range(BLOCKS):
+                column = w * BLOCKS + c
+                nc.scalar.activation(
+                    out=biased[:, c, :],
+                    in_=totals[c],
+                    func=mybir.ActivationFunctionType.Identity,
+                    bias=bias_columns[:, column : column + 1],
+                    scale=1.0,
                 )
+                nc.vector.transpose(out=result[:, c, :], in_=biased[:, c, :])
 
         for w in range(3):
-            for piece in range(RESULT_PIECES):
-                columns = slice(piece * PIECE_COLUMNS, (piece + 1) * PIECE_COLUMNS)
-                nc.sync.dma_start(
-                    out=outs[w][:, piece * PIECE_HEADS : (piece + 1) * PIECE_HEADS, :],
-                    in_=results[w][:, columns].rearrange("s (h d) -> s h d", h=PIECE_HEADS),
-                )
+            nc.sync.dma_start(out=outs[w], in_=results[w][:])

@@ -21,7 +21,7 @@ X_GROUPS = GROUPS // X_PIECES
 GROUP_WORDS = GROUP_K // 2
 GROUPS_PER_BANK = 2
 LOAD_GROUPS = 4
-WEIGHT_SLOTS = 10
+WEIGHT_SLOTS = 16
 PLANES = 4
 PLANE_GROUPS = GROUPS // PLANES
 BLOCKS = FEATURES // P

@@ -95,8 +95,8 @@ def tile_attention_before_k_kernel(
             nc.vector.memset(planes[:].bitcast(I32), 0)
             w_scales.append(planes)
         for w in range(3):
-            for quad in range(4):
-                for r in range(4):
+            for r in range(4):
+                for quad in range(4):
                     nc.gpsimd.dma_start(
                         out=w_scales[w][32 * quad + r : 32 * quad + 4 * PLANES : 4, :]
                         .bitcast(F32)
@@ -180,5 +180,7 @@ def tile_attention_before_k_kernel(
                 )
                 nc.vector.transpose(out=result[:, c, :], in_=biased[:, c, :])
 
-        for w in range(3):
+        for w in range(2):
             nc.sync.dma_start(out=outs[w], in_=results[w][:])
+        for c in range(0, BLOCKS, 2):
+            nc.sync.dma_start(out=outs[2][:, c : c + 2, :], in_=results[2][:, c : c + 2, :])

@@ -24,6 +24,7 @@ LOAD_GROUPS = 4
 WEIGHT_SLOTS = 16
 PLANES = 4
 PLANE_GROUPS = GROUPS // PLANES
+HALF = FEATURES // 2
 BLOCKS = FEATURES // P
 SQUARE = 32
 RUN = P // SQUARE
@@ -146,12 +147,16 @@ def tile_attention_before_k_kernel(
                 totals.append(bank[:, 0:P])
             for first in range(0, GROUPS, LOAD_GROUPS):
                 w_codes = weight_pool.tile([P, LOAD_GROUPS, FEATURES], U32, align_bytes=64)
-                last_load = w == 2 and first == GROUPS - LOAD_GROUPS
-                cut = 1 if last_load else LOAD_GROUPS
-                for part in range(0, LOAD_GROUPS, cut):
+                if w == 2 and first == GROUPS - LOAD_GROUPS:
+                    last = LOAD_GROUPS - 1
+                    cuts = [(part, part + 1, 0, FEATURES) for part in range(last)]
+                    cuts += [(last, last + 1, half, half + HALF) for half in (0, HALF)]
+                else:
+                    cuts = [(0, LOAD_GROUPS, 0, FEATURES)]
+                for part, end, left, right in cuts:
                     nc.sync.dma_start(
-                        out=w_codes[:, part : part + cut, :].bitcast(I32),
-                        in_=word_rows[w][:, first + part : first + part + cut, :].bitcast(I32),
+                        out=w_codes[:, part:end, left:right].bitcast(I32),
+                        in_=word_rows[w][:, first + part : first + end, PACK * left : PACK * right].bitcast(I32),
                     )
                 for g in range(first, first + LOAD_GROUPS):
                     plane = g // PLANE_GROUPS
@@ -169,7 +174,7 @@ def tile_attention_before_k_kernel(
             biased = keep.tile([P, BLOCKS, P], F32, name="biased%d" % w, align_bytes=64)
             result = keep.tile([P, BLOCKS, P], F32, name="result%d" % w, align_bytes=64)
             results.append(result)
-            for c in range(BLOCKS):
+            for c in range(0, BLOCKS, 2):
                 column = w * BLOCKS + c
                 nc.scalar.activation(
                     out=biased[:, c, :],
@@ -178,7 +183,17 @@ def tile_attention_before_k_kernel(
                     bias=bias_columns[:, column : column + 1],
                     scale=1.0,
                 )
-                nc.vector.transpose(out=result[:, c, :], in_=biased[:, c, :])
+                nc.vector.tensor_scalar(
+                    out=biased[:, c + 1, :],
+                    in0=totals[c + 1],
+                    scalar1=bias_columns[:, column + 1 : column + 2],
+                    scalar2=None,
+                    op0=mybir.AluOpType.add,
+                )
+                nc.vector.transpose(
+                    out=result[:, c : c + 2, :].rearrange("p c m -> p (c m)"),
+                    in_=biased[:, c : c + 2, :].rearrange("p c m -> p (c m)"),
+                )
 
         for w in range(2):
             nc.sync.dma_start(out=outs[w], in_=results[w][:])

from contextlib import ExitStack

import concourse.mybir as mybir
from concourse.masks import make_identity

BF16 = mybir.dt.bfloat16
F32 = mybir.dt.float32
I32 = mybir.dt.int32
U32 = mybir.dt.uint32
U8 = mybir.dt.uint8
FP8X4 = mybir.dt.float8_e4m3fn_x4

P = 128
HIDDEN = 16384
FEATURES = 512
PACK = 4
GROUP_K = P * PACK
GROUPS = HIDDEN // GROUP_K
X_PIECES = 4
X_GROUPS = GROUPS // X_PIECES
GROUP_WORDS = GROUP_K // 2
GROUPS_PER_BANK = 2
LOAD_GROUPS = 4
WEIGHT_SLOTS = 16
PLANES = 4
PLANE_GROUPS = GROUPS // PLANES
HALF = FEATURES // 2
BLOCKS = FEATURES // P
SQUARE = 32
RUN = P // SQUARE

FLOPS = 2 * P * HIDDEN * 3 * FEATURES


def tile_attention_before_k_kernel(
    tc,
    hidden_states,
    Wq_words,
    Wq_scales,
    bq,
    Wk_words,
    Wk_scales,
    bk,
    Wv_words,
    Wv_scales,
    bv,
    out_0,
    out_1,
    out_2,
):
    nc = tc.nc
    x = hidden_states.rearrange("b s k -> (b s) k")
    biases = [bq, bk, bv]
    scale_bytes = [Wq_scales, Wk_scales, Wv_scales]
    outs = [
        o.rearrange("b h (a r) d -> (b h a) (r d)", r=RUN).rearrange("(c p) e -> p c e", p=P)
        for o in (out_0, out_1, out_2)
    ]
    word_rows = [w.rearrange("g p n t -> p g (n t)") for w in (Wq_words, Wk_words, Wv_words)]

    with ExitStack() as ctx:
        ctx.enter_context(tc.manual_schedule())
        keep = ctx.enter_context(tc.tile_pool(name="keep", bufs=1))
        x_pool = ctx.enter_context(tc.tile_pool(name="x_pool", bufs=X_PIECES))
        grouped_pool = ctx.enter_context(tc.tile_pool(name="grouped_pool", bufs=2))
        weight_pool = ctx.enter_context(tc.tile_pool(name="weight_pool", bufs=WEIGHT_SLOTS))
        transposed_pool = ctx.enter_context(tc.psum_pool(name="transposed_pool", bufs=4))
        sum_pool = ctx.enter_context(tc.psum_pool(name="sum_pool", bufs=1))

        x_raw = []
        for piece in range(X_PIECES):
            raw = x_pool.tile([P, X_GROUPS * GROUP_K], BF16, name="x_raw")
            nc.sync.dma_start(
                out=raw[:], in_=x[:, piece * X_GROUPS * GROUP_K : (piece + 1) * X_GROUPS * GROUP_K]
            )
            x_raw.append(raw)

        bias_rows = keep.tile([P, P], BF16)
        nc.vector.memset(bias_rows[:], 0.0)
        identity = keep.tile([P, P], F32)
        make_identity(nc, identity[:])
        reorder = keep.tile([P, P], F32)
        nc.vector.tensor_copy(
            out=reorder[:].rearrange("p (r a) -> p r a", r=RUN),
            in_=identity[:].rearrange("p (a r) -> p r a", r=RUN),
        )
        for w in range(3):
            nc.scalar.dma_start(
                out=bias_rows[w * BLOCKS : (w + 1) * BLOCKS, :],
                in_=biases[w].rearrange("(c n) -> c n", c=BLOCKS),
            )

        w_scales = []
        for w in range(3):
            planes = keep.tile([P, PLANE_GROUPS * FEATURES], U8, name="w_scales%d" % w, align_bytes=64)
            nc.vector.memset(planes[:].bitcast(I32), 0)
            w_scales.append(planes)
        for w in range(3):
            for r in range(4):
                for quad in range(4):
                    nc.gpsimd.dma_start(
                        out=w_scales[w][32 * quad + r : 32 * quad + 4 * PLANES : 4, :]
                        .bitcast(F32)
                        .rearrange("plane (g n) -> plane g n", g=PLANE_GROUPS),
                        in_=scale_bytes[w][:, 4 * quad + r, :]
                        .rearrange("(plane g) n -> plane g n", plane=PLANES)
                        .bitcast(F32),
                    )

        x_codes = keep.tile([P, GROUPS, P], U32, align_bytes=64)
        x_scales = keep.tile([P, GROUPS, P], U8, align_bytes=64)
        for piece in range(X_PIECES):
            words = x_raw[piece][:].bitcast(F32)
            grouped = grouped_pool.tile([P, X_GROUPS, P, PACK], BF16, align_bytes=64)
            for first in range(0, X_GROUPS, GROUPS_PER_BANK):
                transposed = transposed_pool.tile([P, GROUPS_PER_BANK, 2, P], F32, name="transposed", tag="turned")
                for g in range(first, first + GROUPS_PER_BANK):
                    for half in range(2):
                        nc.tensor.transpose(
                            out=transposed[:, g - first, half, :],
                            in_=words[:, g * GROUP_WORDS + half : (g + 1) * GROUP_WORDS : 2],
                            identity=reorder[:],
                        )
                nc.scalar.copy(
                    out=grouped[:, first : first + GROUPS_PER_BANK, :, :].bitcast(F32),
                    in_=transposed[:].rearrange("p g half m -> p g m half"),
                )
            piece_groups = slice(piece * X_GROUPS, (piece + 1) * X_GROUPS)
            nc.vector.quantize_mx(
                out=x_codes[:, piece_groups, :].rearrange("p g m -> p (g m)").bitcast(FP8X4),
                scales=x_scales[:, piece_groups, :].rearrange("p g m -> p (g m)"),
                in_=grouped[:].rearrange("p g m t -> p (g m t)"),
            )

        bias_words = keep.tile([P, P], F32)
        nc.vector.tensor_copy(out=bias_words[:], in_=bias_rows[:])
        bias_turned = transposed_pool.tile([P, P], F32, name="bias_turned", tag="turned")
        nc.tensor.transpose(out=bias_turned[:], in_=bias_words[:], identity=identity[:])
        bias_columns = keep.tile([P, 3 * BLOCKS], F32)
        nc.vector.tensor_copy(out=bias_columns[:], in_=bias_turned[:, 0 : 3 * BLOCKS])

        results = []
        for w in range(3):
            totals = []
            for c in range(BLOCKS):
                bank = sum_pool.tile([P, FEATURES], F32, name="bank", tag="bank%d" % c)
                totals.append(bank[:, 0:P])
            for first in range(0, GROUPS, LOAD_GROUPS):
                w_codes = weight_pool.tile([P, LOAD_GROUPS, FEATURES], U32, align_bytes=64)
                if w == 2 and first == GROUPS - LOAD_GROUPS:
                    last = LOAD_GROUPS - 1
                    cuts = [(part, part + 1, 0, FEATURES) for part in range(last)]
                    cuts += [(last, last + 1, half, half + HALF) for half in (0, HALF)]
                else:
                    cuts = [(0, LOAD_GROUPS, 0, FEATURES)]
                for part, end, left, right in cuts:
                    nc.sync.dma_start(
                        out=w_codes[:, part:end, left:right].bitcast(I32),
                        in_=word_rows[w][:, first + part : first + end, PACK * left : PACK * right].bitcast(I32),
                    )
                for g in range(first, first + LOAD_GROUPS):
                    plane = g // PLANE_GROUPS
                    column = (g % PLANE_GROUPS) * FEATURES
                    for c in range(BLOCKS):
                        nc.tensor.matmul_mx(
                            out=totals[c],
                            lhsT=w_codes[:, g - first, c * P : (c + 1) * P].bitcast(FP8X4),
                            lhsT_scale=w_scales[w][4 * plane : P, column + c * P : column + (c + 1) * P],
                            rhs=x_codes[:, g, :].bitcast(FP8X4),
                            rhs_scale=x_scales[:, g, :],
                            start=(g == 0),
                            stop=(g == GROUPS - 1),
                        )
            biased = keep.tile([P, BLOCKS, P], F32, name="biased%d" % w, align_bytes=64)
            result = keep.tile([P, BLOCKS, P], F32, name="result%d" % w, align_bytes=64)
            results.append(result)
            for c in range(0, BLOCKS, 2):
                column = w * BLOCKS + c
                nc.scalar.activation(
                    out=biased[:, c, :],
                    in_=totals[c],
                    func=mybir.ActivationFunctionType.Identity,
                    bias=bias_columns[:, column : column + 1],
                    scale=1.0,
                )
                nc.vector.tensor_scalar(
                    out=biased[:, c + 1, :],
                    in0=totals[c + 1],
                    scalar1=bias_columns[:, column + 1 : column + 2],
                    scalar2=None,
                    op0=mybir.AluOpType.add,
                )
                nc.vector.transpose(
                    out=result[:, c : c + 2, :].rearrange("p c m -> p (c m)"),
                    in_=biased[:, c : c + 2, :].rearrange("p c m -> p (c m)"),
                )

        for w in range(2):
            nc.sync.dma_start(out=outs[w], in_=results[w][:])
        for c in range(0, BLOCKS, 2):
            nc.sync.dma_start(out=outs[2][:, c : c + 2, :], in_=results[2][:, c : c + 2, :])
